import numpy as np
import ml_dtypes


def mxq(x, axis, fmt="e4m3"):
    dtype, down = {"e4m3": (ml_dtypes.float8_e4m3fn, 7), "e5m2": (ml_dtypes.float8_e5m2, 14)}[fmt]
    v = np.moveaxis(np.asarray(x, np.float32).astype(ml_dtypes.bfloat16).astype(np.float64), axis, -1)
    blocks = v.reshape(v.shape[:-1] + (-1, 32))
    amax = np.abs(blocks).max(-1, keepdims=True)
    byte = np.maximum(np.where(amax > 0, np.frexp(amax)[1] - 1 + 127, 0) - down, 1)
    scale = np.exp2(byte - 127.0)
    codes = (blocks / scale).astype(np.float32).astype(dtype).astype(np.float64)
    return np.moveaxis((codes * scale).reshape(v.shape), -1, axis)


WIDE = False


def mx_kscale(k):
    if not WIDE:
        return np.ones(k)
    levels = np.array([10, -10, 5, -5, 0])
    a = np.random.permutation(np.resize(levels, k // 512 * 4)).reshape(k // 512, 4)
    idx = np.arange(k)
    return np.exp2(a[idx // 512, idx % 128 // 32])


BF16 = ml_dtypes.bfloat16


def bf(x):
    return np.asarray(x, np.float32).astype(BF16)


def f64(x):
    return np.asarray(x).astype(np.float64)


E2M1 = np.array([0.0, 0.5, 1.0, 1.5, 2.0, 3.0, 4.0, 6.0, -0.0, -0.5, -1.0, -1.5, -2.0, -3.0, -4.0, -6.0])


def pack_weight(w, fmt):
    k, n = w.shape
    w = f64(bf(w)).reshape(k // 32, 32, n)
    amax = np.abs(w).max(1)
    if fmt == "e4m3":
        byte = np.frexp(amax)[1] - 1 + 127 - 7
    else:
        mant, ex = np.frexp(amax / 6.0)
        byte = np.where(mant > 0.5, ex, ex - 1) + 127
    byte = np.clip(np.where(amax > 0, byte, 1), 1, 254)
    scaled = (w * np.exp2(127.0 - byte)[:, None, :]).reshape(k, n).astype(np.float32)
    by_word = np.ascontiguousarray(scaled.reshape(k // 512, 128, 4, n).transpose(0, 1, 3, 2))
    if fmt == "e4m3":
        words = by_word.astype(ml_dtypes.float8_e4m3fn).view(np.uint8)
    else:
        c = by_word.astype(ml_dtypes.float4_e2m1fn).view(np.uint8) & 0xF
        words = c[..., 0::2] | (c[..., 1::2] << 4)
    return np.ascontiguousarray(words), np.ascontiguousarray(byte.astype(np.uint8).reshape(k // 512, 16, n))


def unpack_weight(words, scales, fmt):
    g, p, n, _ = words.shape
    if fmt == "e4m3":
        vals = np.ascontiguousarray(words).view(ml_dtypes.float8_e4m3fn).astype(np.float64)
    else:
        nib = np.empty((g, p, n, 4), np.uint8)
        nib[..., 0::2] = words & 0xF
        nib[..., 1::2] = words >> 4
        vals = E2M1[nib]
    vals = vals * np.repeat(np.exp2(scales.astype(np.float64) - 127.0), 8, axis=1)[..., None]
    return vals.transpose(0, 1, 3, 2).reshape(g * 512, n)


B, DIN, DOUT = 128, 8192, 512
FMT = "e4m3"


def sigmoid(v):
    return 1.0 / (1.0 + np.exp(-v))


def setup_inputs():
    s, t = mx_kscale(DIN), mx_kscale(DOUT)
    inp = {"x": bf(np.random.standard_normal((B, DIN)) * s),
           "h": bf(np.random.standard_normal((B, DOUT)) * t),
           "c": bf(np.random.standard_normal((B, DOUT)))}
    for n in "ifgo":
        inp["Wx" + n + "_words"], inp["Wx" + n + "_scales"] = pack_weight(np.random.standard_normal((DIN, DOUT)) * 0.7 / np.sqrt(DIN) / s[:, None], FMT)
        inp["Wh" + n + "_words"], inp["Wh" + n + "_scales"] = pack_weight(np.random.standard_normal((DOUT, DOUT)) * 0.7 / np.sqrt(DOUT) / t[:, None], FMT)
        inp["bx" + n] = bf(np.random.standard_normal(DOUT) * 0.3)
        inp["bh" + n] = bf(np.random.standard_normal(DOUT) * 0.3)
    return inp


def reference(x, h, c,
              Wxi_words, Wxi_scales, Whi_words, Whi_scales, bxi, bhi,
              Wxf_words, Wxf_scales, Whf_words, Whf_scales, bxf, bhf,
              Wxg_words, Wxg_scales, Whg_words, Whg_scales, bxg, bhg,
              Wxo_words, Wxo_scales, Who_words, Who_scales, bxo, bho):
    Wx = np.concatenate([unpack_weight(Wxi_words, Wxi_scales, FMT), unpack_weight(Wxf_words, Wxf_scales, FMT), unpack_weight(Wxg_words, Wxg_scales, FMT), unpack_weight(Wxo_words, Wxo_scales, FMT)], axis=1)
    Wh = np.concatenate([unpack_weight(Whi_words, Whi_scales, FMT), unpack_weight(Whf_words, Whf_scales, FMT), unpack_weight(Whg_words, Whg_scales, FMT), unpack_weight(Who_words, Who_scales, FMT)], axis=1)
    b = np.concatenate([f64(bxi) + f64(bhi), f64(bxf) + f64(bhf), f64(bxg) + f64(bhg), f64(bxo) + f64(bho)])
    z = (mxq(f64(x), 1, "e4m3") @ Wx) + (mxq(f64(h), 1, "e4m3") @ Wh) + b
    zi, zf, zg, zo = np.split(z, 4, axis=1)
    i = sigmoid(zi)
    f = sigmoid(zf)
    g = np.tanh(zg)
    o = sigmoid(zo)
    c_new = f * f64(c) + i * g
    h_new = o * np.tanh(c_new)
    return (h_new, c_new)

@@ -1,0 +1,194 @@
+from contextlib import ExitStack
+
+import concourse.masks as masks
+import concourse.mybir as mybir
+
+F32 = mybir.dt.float32
+BF16 = mybir.dt.bfloat16
+I32 = mybir.dt.int32
+U32 = mybir.dt.uint32
+U8 = mybir.dt.uint8
+FP8X4 = mybir.dt.float8_e4m3fn_x4
+ACT = mybir.ActivationFunctionType
+
+P = 128
+PACK = 4
+K_PASS = P * PACK
+DIN = 8192
+DOUT = 512
+X_PASSES = DIN // K_PASS
+H_PASS = X_PASSES
+PASSES = X_PASSES + 1
+CHUNK = 4
+BANK_PASSES = 2
+PAIRS = 2
+PASS_WORDS = K_PASS // 2
+QUADRANT = 32
+QUADRANT_ROWS = 4
+assert X_PASSES // CHUNK == QUADRANT_ROWS
+
+GATES = 4
+GATE_I, GATE_F, GATE_G, GATE_O = range(GATES)
+GATE_FUNC = (ACT.Sigmoid, ACT.Sigmoid, ACT.Tanh, ACT.Sigmoid)
+
+FLOPS = 2 * P * (DIN + DOUT) * GATES * DOUT
+
+
+def tile_lstmcell_k_kernel(
+    tc, x, h, c,
+    Wxi_words, Wxi_scales, Whi_words, Whi_scales, bxi, bhi,
+    Wxf_words, Wxf_scales, Whf_words, Whf_scales, bxf, bhf,
+    Wxg_words, Wxg_scales, Whg_words, Whg_scales, bxg, bhg,
+    Wxo_words, Wxo_scales, Who_words, Who_scales, bxo, bho,
+    out_0, out_1,
+):
+    nc = tc.nc
+    wx_words_in = (Wxi_words, Wxf_words, Wxg_words, Wxo_words)
+    wx_scales_in = (Wxi_scales, Wxf_scales, Wxg_scales, Wxo_scales)
+    wh_words_in = (Whi_words, Whf_words, Whg_words, Who_words)
+    wh_scales_in = (Whi_scales, Whf_scales, Whg_scales, Who_scales)
+    bx_in = (bxi, bxf, bxg, bxo)
+    bh_in = (bhi, bhf, bhg, bho)
+
+    with ExitStack() as ctx:
+        keep = ctx.enter_context(tc.tile_pool(name="keep", bufs=1))
+        sums = ctx.enter_context(tc.psum_pool(name="sums", bufs=1))
+        plain = ctx.enter_context(tc.psum_pool(name="plain", bufs=4))
+
+        c_sb = keep.tile([P, DOUT], BF16)
+        w_words = [
+            keep.tile([P, PASSES, DOUT], U32, align_bytes=64, name="w_words_%d" % n)
+            for n in range(GATES)
+        ]
+        wx_planes = [
+            keep.tile([P, X_PASSES, DOUT], U8, align_bytes=64, name="wx_planes_%d" % n)
+            for n in range(GATES)
+        ]
+        wh_plane = [
+            keep.tile([P, DOUT], U8, align_bytes=64, name="wh_plane_%d" % n)
+            for n in range(GATES)
+        ]
+        xh_codes = keep.tile([P, PASSES, P], U32, align_bytes=64)
+        xh_planes = keep.tile([P, PASSES, P], U8, align_bytes=64)
+        identity = keep.tile([P, P], F32)
+        ones = keep.tile([P, P], BF16)
+        bias_rows = keep.tile([P, GATES, DOUT], BF16)
+
+        for n in range(GATES):
+            nc.vector.memset(wx_planes[n][:].bitcast(I32), 0)
+            nc.vector.memset(wh_plane[n][:].bitcast(I32), 0)
+        nc.vector.memset(bias_rows[:], 0.0)
+        nc.vector.memset(ones[:], 1.0)
+        masks.make_identity(nc, identity[:])
+
+        with tc.tile_pool(name="arrive", bufs=1) as arrive, tc.tile_pool(name="stage", bufs=2) as stage:
+            xh = arrive.tile([P, DIN + DOUT], BF16)
+
+            for first in range(0, X_PASSES, CHUNK):
+                cols = slice(first * K_PASS, (first + CHUNK) * K_PASS)
+                nc.sync.dma_start(out=xh[:, cols], in_=x[:, cols])
+            nc.sync.dma_start(out=xh[:, DIN:], in_=h)
+            nc.sync.dma_start(out=c_sb[:], in_=c)
+            for n in range(GATES):
+                nc.sync.dma_start(out=bias_rows[0:1, n, :], in_=bx_in[n].unsqueeze(0))
+                nc.sync.dma_start(out=bias_rows[1:2, n, :], in_=bh_in[n].unsqueeze(0))
+                wx_rows = wx_words_in[n].rearrange("g p n t -> p g (n t)")
+                wh_scale_rows = wh_scales_in[n].rearrange(
+                    "g (q r) n -> r q (g n)", r=QUADRANT_ROWS
+                )
+                for first in range(0, X_PASSES, CHUNK):
+                    r = first // CHUNK
+                    nc.sync.dma_start(
+                        out=wh_plane[n][QUADRANT_ROWS * n + r : P : QUADRANT, :].bitcast(I32),
+                        in_=wh_scale_rows[r].bitcast(I32),
+                    )
+                    nc.sync.dma_start(
+                        out=w_words[n][:, first : first + CHUNK, :].bitcast(I32),
+                        in_=wx_rows[:, first : first + CHUNK, :].bitcast(I32),
+                    )
+                nc.sync.dma_start(
+                    out=w_words[n][:, H_PASS, :].bitcast(I32),
+                    in_=wh_words_in[n].rearrange("g p n t -> p (g n t)").bitcast(I32),
+                )
+
+            for n in range(GATES):
+                rows = wx_scales_in[n].rearrange("g (q r) n -> r q g n", r=QUADRANT_ROWS)
+                for r in range(QUADRANT_ROWS):
+                    nc.gpsimd.dma_start(
+                        out=wx_planes[n][QUADRANT_ROWS * n + r : P : QUADRANT, :, :].bitcast(F32),
+                        in_=rows[r].bitcast(F32),
+                    )
+
+            xh_pairs = xh[:].bitcast(F32)
+            banks_done = 0
+            for first in range(0, PASSES, CHUNK):
+                count = min(CHUNK, PASSES - first)
+                grouped = stage.tile([P, CHUNK, P, PACK], BF16, align_bytes=64)
+                for lead in range(0, count, BANK_PASSES):
+                    here = min(BANK_PASSES, count - lead)
+                    flipped = plain.tile([P, BANK_PASSES, PAIRS, P], F32, tag="plain")
+                    for j in range(here):
+                        start = (first + lead + j) * PASS_WORDS
+                        for u in range(PAIRS):
+                            nc.tensor.transpose(
+                                flipped[:, j, u, :],
+                                xh_pairs[:, start + u : start + PASS_WORDS : PAIRS],
+                                identity[:],
+                            )
+                    copy_out = nc.vector.tensor_copy if banks_done % 2 == 0 else nc.scalar.copy
+                    copy_out(
+                        out=grouped[:, lead : lead + here, :, :].bitcast(F32),
+                        in_=flipped[:, 0:here, :, :].rearrange("p j u b -> p j b u"),
+                    )
+                    banks_done += 1
+                nc.vector.quantize_mx(
+                    out=xh_codes[:, first : first + count, :]
+                    .rearrange("p g b -> p (g b)")
+                    .bitcast(FP8X4),
+                    scales=xh_planes[:, first : first + count, :].rearrange("p g b -> p (g b)"),
+                    in_=grouped[:, 0:count, :, :].rearrange("p g b t -> p (g b t)"),
+                )
+
+        late = ctx.enter_context(tc.tile_pool(name="late", bufs=1))
+        gate = []
+        for n in range(GATES):
+            spread = plain.tile([P, DOUT], F32, tag="plain")
+            nc.tensor.matmul(
+                out=spread[:], lhsT=ones[:], rhs=bias_rows[:, n, :], start=True, stop=True
+            )
+            bias = late.tile([P, DOUT], F32, name="bias_%d" % n)
+            nc.scalar.copy(out=bias[:], in_=spread[:])
+
+            z_sum = sums.tile([P, DOUT], F32, name="z_sum_%d" % n)
+            for g in range(PASSES):
+                w_plane = wh_plane[n][:] if g == H_PASS else wx_planes[n][:, g, :]
+                nc.tensor.matmul_mx(
+                    out=z_sum[:],
+                    lhsT=xh_codes[:, g, :].bitcast(FP8X4),
+                    lhsT_scale=xh_planes[:, g, :],
+                    rhs=w_words[n][:, g, :].bitcast(FP8X4),
+                    rhs_scale=w_plane[QUADRANT_ROWS * n : P, :],
+                    start=(g == 0),
+                    stop=(g == PASSES - 1),
+                )
+            z = late.tile([P, DOUT], F32, name="z_%d" % n)
+            nc.vector.tensor_add(out=z[:], in0=z_sum[:], in1=bias[:])
+            value = late.tile([P, DOUT], F32, name="gate_%d" % n)
+            nc.scalar.activation(out=value[:], in_=z[:], func=GATE_FUNC[n])
+            gate.append(value)
+
+            if n == GATE_F:
+                kept = late.tile([P, DOUT], F32)
+                nc.vector.tensor_mul(out=kept[:], in0=gate[GATE_F][:], in1=c_sb[:])
+            if n == GATE_G:
+                fresh = late.tile([P, DOUT], F32)
+                nc.vector.tensor_mul(out=fresh[:], in0=gate[GATE_I][:], in1=gate[GATE_G][:])
+                c_new = late.tile([P, DOUT], F32)
+                nc.vector.tensor_add(out=c_new[:], in0=kept[:], in1=fresh[:])
+                tanh_c = late.tile([P, DOUT], F32)
+                nc.scalar.activation(out=tanh_c[:], in_=c_new[:], func=ACT.Tanh)
+                nc.scalar.dma_start(out=out_1, in_=c_new[:])
+            if n == GATE_O:
+                h_new = late.tile([P, DOUT], F32)
+                nc.vector.tensor_mul(out=h_new[:], in0=gate[GATE_O][:], in1=tanh_c[:])
+                nc.sync.dma_start(out=out_0, in_=h_new[:])

@@ -14,18 +14,22 @@ ACT = mybir.ActivationFunctionType
 P = 128
 PACK = 4
 K_PASS = P * PACK
+BLOCK = 32
+BLOCK_PARTS = BLOCK // PACK
+PASS_BLOCKS = K_PASS // BLOCK
 DIN = 8192
 DOUT = 512
-X_PASSES = DIN // K_PASS
+CHUNK_PASSES = 4
+CHUNKS = DIN // (CHUNK_PASSES * K_PASS)
+X_PASSES = CHUNKS * CHUNK_PASSES
 H_PASS = X_PASSES
 PASSES = X_PASSES + 1
-CHUNK = 4
 BANK_PASSES = 2
 PAIRS = 2
 PASS_WORDS = K_PASS // 2
 QUADRANT = 32
-QUADRANT_ROWS = 4
-assert X_PASSES // CHUNK == QUADRANT_ROWS
+QUADRANTS = P // QUADRANT
+QUADRANT_ROWS = PASS_BLOCKS // QUADRANTS
 
 GATES = 4
 GATE_I, GATE_F, GATE_G, GATE_O = range(GATES)
@@ -61,7 +65,7 @@ def tile_lstmcell_k_kernel(
             for n in range(GATES)
         ]
         wx_planes = [
-            keep.tile([P, X_PASSES, DOUT], U8, align_bytes=64, name="wx_planes_%d" % n)
+            keep.tile([P, CHUNK_PASSES, DOUT], U8, align_bytes=64, name="wx_planes_%d" % n)
             for n in range(GATES)
         ]
         wh_plane = [
@@ -74,56 +78,79 @@ def tile_lstmcell_k_kernel(
         ones = keep.tile([P, P], BF16)
         bias_rows = keep.tile([P, GATES, DOUT], BF16)
 
+        nc.vector.memset(bias_rows[:], 0.0)
+        nc.vector.memset(ones[:], 1.0)
         for n in range(GATES):
             nc.vector.memset(wx_planes[n][:].bitcast(I32), 0)
             nc.vector.memset(wh_plane[n][:].bitcast(I32), 0)
-        nc.vector.memset(bias_rows[:], 0.0)
-        nc.vector.memset(ones[:], 1.0)
         masks.make_identity(nc, identity[:])
 
         with tc.tile_pool(name="arrive", bufs=1) as arrive, tc.tile_pool(name="stage", bufs=2) as stage:
-            xh = arrive.tile([P, DIN + DOUT], BF16)
+            x_sb = arrive.tile([P, CHUNKS, PASS_BLOCKS, CHUNK_PASSES, BLOCK], BF16)
+            xh_passes = arrive.tile([P, PASSES, PASS_BLOCKS, BLOCK], BF16)
 
-            for first in range(0, X_PASSES, CHUNK):
-                cols = slice(first * K_PASS, (first + CHUNK) * K_PASS)
-                nc.sync.dma_start(out=xh[:, cols], in_=x[:, cols])
-            nc.sync.dma_start(out=xh[:, DIN:], in_=h)
-            nc.sync.dma_start(out=c_sb[:], in_=c)
+            big_loads = []
+            x_chunks = x.rearrange("b (j e) -> b j e", j=CHUNKS)
+            for j in range(CHUNKS):
+                big_loads.append((x_sb[:, j].rearrange("b s c e -> b (s c e)"), x_chunks[:, j, :]))
+            big_loads.append((xh_passes[:, H_PASS].rearrange("b s e -> b (s e)"), h))
+            big_loads.append((c_sb[:], c))
             for n in range(GATES):
-                nc.sync.dma_start(out=bias_rows[0:1, n, :], in_=bx_in[n].unsqueeze(0))
-                nc.sync.dma_start(out=bias_rows[1:2, n, :], in_=bh_in[n].unsqueeze(0))
-                wx_rows = wx_words_in[n].rearrange("g p n t -> p g (n t)")
-                wh_scale_rows = wh_scales_in[n].rearrange(
-                    "g (q r) n -> r q (g n)", r=QUADRANT_ROWS
-                )
-                for first in range(0, X_PASSES, CHUNK):
-                    r = first // CHUNK
-                    nc.sync.dma_start(
-                        out=wh_plane[n][QUADRANT_ROWS * n + r : P : QUADRANT, :].bitcast(I32),
-                        in_=wh_scale_rows[r].bitcast(I32),
+                wx_blocks = (
+                    wx_words_in[n]
+                    .rearrange("g p n t -> (g p) (n t)")
+                    .rearrange(
+                        "(j s c i) b -> j c s i b",
+                        j=CHUNKS, s=PASS_BLOCKS, c=CHUNK_PASSES, i=BLOCK_PARTS,
                     )
-                    nc.sync.dma_start(
-                        out=w_words[n][:, first : first + CHUNK, :].bitcast(I32),
-                        in_=wx_rows[:, first : first + CHUNK, :].bitcast(I32),
-                    )
-                nc.sync.dma_start(
-                    out=w_words[n][:, H_PASS, :].bitcast(I32),
-                    in_=wh_words_in[n].rearrange("g p n t -> p (g n t)").bitcast(I32),
                 )
+                for j in range(CHUNKS):
+                    for cc in range(CHUNK_PASSES):
+                        big_loads.append((
+                            w_words[n][:, j * CHUNK_PASSES + cc, :].bitcast(I32),
+                            wx_blocks[j, cc].bitcast(I32),
+                        ))
+                big_loads.append((
+                    w_words[n][:, H_PASS, :].bitcast(I32),
+                    wh_words_in[n].rearrange("g p n t -> p (g n t)").bitcast(I32),
+                ))
 
+            small_loads = []
             for n in range(GATES):
-                rows = wx_scales_in[n].rearrange("g (q r) n -> r q g n", r=QUADRANT_ROWS)
+                wx_rows = wx_scales_in[n].rearrange(
+                    "(j q) (r c) n -> q j r (c n)", q=QUADRANTS, c=CHUNK_PASSES
+                )
+                for q in range(QUADRANTS):
+                    small_loads.append((
+                        wx_planes[n][q * QUADRANT : q * QUADRANT + PASS_BLOCKS, :, :]
+                        .rearrange("p c n -> p (c n)")
+                        .bitcast(I32),
+                        wx_rows[q].bitcast(I32),
+                    ))
+                small_loads.append((bias_rows[0:1, n, :], bx_in[n].unsqueeze(0)))
+                small_loads.append((bias_rows[1:2, n, :], bh_in[n].unsqueeze(0)))
+                wh_rows = wh_scales_in[n].rearrange("g (q r) n -> r q (g n)", r=QUADRANT_ROWS)
                 for r in range(QUADRANT_ROWS):
-                    nc.gpsimd.dma_start(
-                        out=wx_planes[n][QUADRANT_ROWS * n + r : P : QUADRANT, :, :].bitcast(F32),
-                        in_=rows[r].bitcast(F32),
-                    )
+                    small_loads.append((
+                        wh_plane[n][r:P:QUADRANT, :].bitcast(I32), wh_rows[r].bitcast(I32)
+                    ))
 
-            xh_pairs = xh[:].bitcast(F32)
+            assert len(small_loads) <= len(big_loads)
+            for turn in range(len(big_loads)):
+                nc.sync.dma_start(out=big_loads[turn][0], in_=big_loads[turn][1])
+                if turn < len(small_loads):
+                    nc.sync.dma_start(out=small_loads[turn][0], in_=small_loads[turn][1])
+
+            xh_pairs = xh_passes[:].rearrange("b g s e -> b (g s e)").bitcast(F32)
             banks_done = 0
-            for first in range(0, PASSES, CHUNK):
-                count = min(CHUNK, PASSES - first)
-                grouped = stage.tile([P, CHUNK, P, PACK], BF16, align_bytes=64)
+            for first in range(0, PASSES, CHUNK_PASSES):
+                count = min(CHUNK_PASSES, PASSES - first)
+                if first < X_PASSES:
+                    nc.vector.tensor_copy(
+                        out=xh_passes[:, first : first + count, :, :],
+                        in_=x_sb[:, first // CHUNK_PASSES].rearrange("b s c e -> b c s e"),
+                    )
+                grouped = stage.tile([P, CHUNK_PASSES, P, PACK], BF16, align_bytes=64)
                 for lead in range(0, count, BANK_PASSES):
                     here = min(BANK_PASSES, count - lead)
                     flipped = plain.tile([P, BANK_PASSES, PAIRS, P], F32, tag="plain")
@@ -161,13 +188,18 @@ def tile_lstmcell_k_kernel(
 
             z_sum = sums.tile([P, DOUT], F32, name="z_sum_%d" % n)
             for g in range(PASSES):
-                w_plane = wh_plane[n][:] if g == H_PASS else wx_planes[n][:, g, :]
+                if g == H_PASS:
+                    w_plane = wh_plane[n][:]
+                else:
+                    w_plane = wx_planes[n][
+                        QUADRANT_ROWS * (g // CHUNK_PASSES) : P, g % CHUNK_PASSES, :
+                    ]
                 nc.tensor.matmul_mx(
                     out=z_sum[:],
                     lhsT=xh_codes[:, g, :].bitcast(FP8X4),
                     lhsT_scale=xh_planes[:, g, :],
                     rhs=w_words[n][:, g, :].bitcast(FP8X4),
-                    rhs_scale=w_plane[QUADRANT_ROWS * n : P, :],
+                    rhs_scale=w_plane,
                     start=(g == 0),
                     stop=(g == PASSES - 1),
                 )

@@ -14,22 +14,18 @@ ACT = mybir.ActivationFunctionType
 P = 128
 PACK = 4
 K_PASS = P * PACK
-BLOCK = 32
-BLOCK_PARTS = BLOCK // PACK
-PASS_BLOCKS = K_PASS // BLOCK
 DIN = 8192
 DOUT = 512
-CHUNK_PASSES = 4
-CHUNKS = DIN // (CHUNK_PASSES * K_PASS)
-X_PASSES = CHUNKS * CHUNK_PASSES
+X_PASSES = DIN // K_PASS
 H_PASS = X_PASSES
 PASSES = X_PASSES + 1
+CHUNK = 4
 BANK_PASSES = 2
 PAIRS = 2
 PASS_WORDS = K_PASS // 2
 QUADRANT = 32
-QUADRANTS = P // QUADRANT
-QUADRANT_ROWS = PASS_BLOCKS // QUADRANTS
+QUADRANT_ROWS = 4
+assert X_PASSES // CHUNK == QUADRANT_ROWS
 
 GATES = 4
 GATE_I, GATE_F, GATE_G, GATE_O = range(GATES)
@@ -56,18 +52,17 @@ def tile_lstmcell_k_kernel(
 
     with ExitStack() as ctx:
         keep = ctx.enter_context(tc.tile_pool(name="keep", bufs=1))
+        stage = ctx.enter_context(tc.tile_pool(name="stage", bufs=2))
         sums = ctx.enter_context(tc.psum_pool(name="sums", bufs=1))
         plain = ctx.enter_context(tc.psum_pool(name="plain", bufs=4))
 
+        xh = keep.tile([P, DIN + DOUT], BF16)
         c_sb = keep.tile([P, DOUT], BF16)
         w_words = [
             keep.tile([P, PASSES, DOUT], U32, align_bytes=64, name="w_words_%d" % n)
             for n in range(GATES)
         ]
-        wx_planes = [
-            keep.tile([P, CHUNK_PASSES, DOUT], U8, align_bytes=64, name="wx_planes_%d" % n)
-            for n in range(GATES)
-        ]
+        wx_planes = keep.tile([P, X_PASSES, DOUT], U8, align_bytes=64)
         wh_plane = [
             keep.tile([P, DOUT], U8, align_bytes=64, name="wh_plane_%d" % n)
             for n in range(GATES)
@@ -78,112 +73,84 @@ def tile_lstmcell_k_kernel(
         ones = keep.tile([P, P], BF16)
         bias_rows = keep.tile([P, GATES, DOUT], BF16)
 
+        nc.vector.memset(wx_planes[:].bitcast(I32), 0)
+        for n in range(GATES):
+            nc.vector.memset(wh_plane[n][:].bitcast(I32), 0)
         nc.vector.memset(bias_rows[:], 0.0)
         nc.vector.memset(ones[:], 1.0)
-        for n in range(GATES):
-            nc.vector.memset(wx_planes[n][:].bitcast(I32), 0)
-            nc.vector.memset(wh_plane[n][:].bitcast(I32), 0)
         masks.make_identity(nc, identity[:])
 
-        with tc.tile_pool(name="arrive", bufs=1) as arrive, tc.tile_pool(name="stage", bufs=2) as stage:
-            x_sb = arrive.tile([P, CHUNKS, PASS_BLOCKS, CHUNK_PASSES, BLOCK], BF16)
-            xh_passes = arrive.tile([P, PASSES, PASS_BLOCKS, BLOCK], BF16)
+        for n in range(GATES):
+            rows = wx_scales_in[n].rearrange("g (q r) n -> r q g n", r=QUADRANT_ROWS)
+            for r in range(QUADRANT_ROWS):
+                landing = wx_planes[QUADRANT_ROWS * n + r : P : QUADRANT, :, :]
+                if n < GATES // 2:
+                    nc.sync.dma_start(out=landing.bitcast(I32), in_=rows[r].bitcast(I32))
+                else:
+                    nc.gpsimd.dma_start(out=landing.bitcast(F32), in_=rows[r].bitcast(F32))
 
-            big_loads = []
-            x_chunks = x.rearrange("b (j e) -> b j e", j=CHUNKS)
-            for j in range(CHUNKS):
-                big_loads.append((x_sb[:, j].rearrange("b s c e -> b (s c e)"), x_chunks[:, j, :]))
-            big_loads.append((xh_passes[:, H_PASS].rearrange("b s e -> b (s e)"), h))
-            big_loads.append((c_sb[:], c))
-            for n in range(GATES):
-                wx_blocks = (
-                    wx_words_in[n]
-                    .rearrange("g p n t -> (g p) (n t)")
-                    .rearrange(
-                        "(j s c i) b -> j c s i b",
-                        j=CHUNKS, s=PASS_BLOCKS, c=CHUNK_PASSES, i=BLOCK_PARTS,
-                    )
+        for first in range(0, X_PASSES, CHUNK):
+            cols = slice(first * K_PASS, (first + CHUNK) * K_PASS)
+            nc.sync.dma_start(out=xh[:, cols], in_=x[:, cols])
+        nc.sync.dma_start(out=xh[:, DIN:], in_=h)
+        nc.sync.dma_start(out=c_sb[:], in_=c)
+        for n in range(GATES):
+            nc.sync.dma_start(out=bias_rows[0:1, n, :], in_=bx_in[n].unsqueeze(0))
+            nc.sync.dma_start(out=bias_rows[1:2, n, :], in_=bh_in[n].unsqueeze(0))
+            wx_rows = wx_words_in[n].rearrange("g p n t -> p g (n t)")
+            wh_scale_rows = wh_scales_in[n].rearrange("g (q r) n -> r q (g n)", r=QUADRANT_ROWS)
+            for first in range(0, X_PASSES, CHUNK):
+                r = first // CHUNK
+                nc.sync.dma_start(
+                    out=wh_plane[n][r:P:QUADRANT, :].bitcast(I32),
+                    in_=wh_scale_rows[r].bitcast(I32),
                 )
-                for j in range(CHUNKS):
-                    for cc in range(CHUNK_PASSES):
-                        big_loads.append((
-                            w_words[n][:, j * CHUNK_PASSES + cc, :].bitcast(I32),
-                            wx_blocks[j, cc].bitcast(I32),
-                        ))
-                big_loads.append((
-                    w_words[n][:, H_PASS, :].bitcast(I32),
-                    wh_words_in[n].rearrange("g p n t -> p (g n t)").bitcast(I32),
-                ))
-
-            small_loads = []
-            for n in range(GATES):
-                wx_rows = wx_scales_in[n].rearrange(
-                    "(j q) (r c) n -> q j r (c n)", q=QUADRANTS, c=CHUNK_PASSES
+                nc.sync.dma_start(
+                    out=w_words[n][:, first : first + CHUNK, :].bitcast(I32),
+                    in_=wx_rows[:, first : first + CHUNK, :].bitcast(I32),
                 )
-                for q in range(QUADRANTS):
-                    small_loads.append((
-                        wx_planes[n][q * QUADRANT : q * QUADRANT + PASS_BLOCKS, :, :]
-                        .rearrange("p c n -> p (c n)")
-                        .bitcast(I32),
-                        wx_rows[q].bitcast(I32),
-                    ))
-                small_loads.append((bias_rows[0:1, n, :], bx_in[n].unsqueeze(0)))
-                small_loads.append((bias_rows[1:2, n, :], bh_in[n].unsqueeze(0)))
-                wh_rows = wh_scales_in[n].rearrange("g (q r) n -> r q (g n)", r=QUADRANT_ROWS)
-                for r in range(QUADRANT_ROWS):
-                    small_loads.append((
-                        wh_plane[n][r:P:QUADRANT, :].bitcast(I32), wh_rows[r].bitcast(I32)
-                    ))
+            nc.sync.dma_start(
+                out=w_words[n][:, H_PASS, :].bitcast(I32),
+                in_=wh_words_in[n].rearrange("g p n t -> p (g n t)").bitcast(I32),
+            )
 
-            assert len(small_loads) <= len(big_loads)
-            for turn in range(len(big_loads)):
-                nc.sync.dma_start(out=big_loads[turn][0], in_=big_loads[turn][1])
-                if turn < len(small_loads):
-                    nc.sync.dma_start(out=small_loads[turn][0], in_=small_loads[turn][1])
-
-            xh_pairs = xh_passes[:].rearrange("b g s e -> b (g s e)").bitcast(F32)
-            banks_done = 0
-            for first in range(0, PASSES, CHUNK_PASSES):
-                count = min(CHUNK_PASSES, PASSES - first)
-                if first < X_PASSES:
-                    nc.vector.tensor_copy(
-                        out=xh_passes[:, first : first + count, :, :],
-                        in_=x_sb[:, first // CHUNK_PASSES].rearrange("b s c e -> b c s e"),
-                    )
-                grouped = stage.tile([P, CHUNK_PASSES, P, PACK], BF16, align_bytes=64)
-                for lead in range(0, count, BANK_PASSES):
-                    here = min(BANK_PASSES, count - lead)
-                    flipped = plain.tile([P, BANK_PASSES, PAIRS, P], F32, tag="plain")
-                    for j in range(here):
-                        start = (first + lead + j) * PASS_WORDS
-                        for u in range(PAIRS):
-                            nc.tensor.transpose(
-                                flipped[:, j, u, :],
-                                xh_pairs[:, start + u : start + PASS_WORDS : PAIRS],
-                                identity[:],
-                            )
-                    copy_out = nc.vector.tensor_copy if banks_done % 2 == 0 else nc.scalar.copy
-                    copy_out(
-                        out=grouped[:, lead : lead + here, :, :].bitcast(F32),
-                        in_=flipped[:, 0:here, :, :].rearrange("p j u b -> p j b u"),
-                    )
-                    banks_done += 1
-                nc.vector.quantize_mx(
-                    out=xh_codes[:, first : first + count, :]
-                    .rearrange("p g b -> p (g b)")
-                    .bitcast(FP8X4),
-                    scales=xh_planes[:, first : first + count, :].rearrange("p g b -> p (g b)"),
-                    in_=grouped[:, 0:count, :, :].rearrange("p g b t -> p (g b t)"),
+        xh_pairs = xh[:].bitcast(F32)
+        banks_done = 0
+        for first in range(0, PASSES, CHUNK):
+            count = min(CHUNK, PASSES - first)
+            grouped = stage.tile([P, CHUNK, P, PACK], BF16, align_bytes=64)
+            for lead in range(0, count, BANK_PASSES):
+                here = min(BANK_PASSES, count - lead)
+                flipped = plain.tile([P, BANK_PASSES, PAIRS, P], F32, tag="plain")
+                for j in range(here):
+                    start = (first + lead + j) * PASS_WORDS
+                    for u in range(PAIRS):
+                        nc.tensor.transpose(
+                            flipped[:, j, u, :],
+                            xh_pairs[:, start + u : start + PASS_WORDS : PAIRS],
+                            identity[:],
+                        )
+                copy_out = nc.vector.tensor_copy if banks_done % 2 == 0 else nc.scalar.copy
+                copy_out(
+                    out=grouped[:, lead : lead + here, :, :].bitcast(F32),
+                    in_=flipped[:, 0:here, :, :].rearrange("p j u b -> p j b u"),
                 )
+                banks_done += 1
+            nc.vector.quantize_mx(
+                out=xh_codes[:, first : first + count, :]
+                .rearrange("p g b -> p (g b)")
+                .bitcast(FP8X4),
+                scales=xh_planes[:, first : first + count, :].rearrange("p g b -> p (g b)"),
+                in_=grouped[:, 0:count, :, :].rearrange("p g b t -> p (g b t)"),
+            )
 
-        late = ctx.enter_context(tc.tile_pool(name="late", bufs=1))
         gate = []
         for n in range(GATES):
             spread = plain.tile([P, DOUT], F32, tag="plain")
             nc.tensor.matmul(
                 out=spread[:], lhsT=ones[:], rhs=bias_rows[:, n, :], start=True, stop=True
             )
-            bias = late.tile([P, DOUT], F32, name="bias_%d" % n)
+            bias = keep.tile([P, DOUT], F32, name="bias_%d" % n)
             nc.scalar.copy(out=bias[:], in_=spread[:])
 
             z_sum = sums.tile([P, DOUT], F32, name="z_sum_%d" % n)
@@ -191,9 +158,7 @@ def tile_lstmcell_k_kernel(
                 if g == H_PASS:
                     w_plane = wh_plane[n][:]
                 else:
-                    w_plane = wx_planes[n][
-                        QUADRANT_ROWS * (g // CHUNK_PASSES) : P, g % CHUNK_PASSES, :
-                    ]
+                    w_plane = wx_planes[QUADRANT_ROWS * n : P, g, :]
                 nc.tensor.matmul_mx(
                     out=z_sum[:],
                     lhsT=xh_codes[:, g, :].bitcast(FP8X4),
@@ -203,24 +168,24 @@ def tile_lstmcell_k_kernel(
                     start=(g == 0),
                     stop=(g == PASSES - 1),
                 )
-            z = late.tile([P, DOUT], F32, name="z_%d" % n)
+            z = keep.tile([P, DOUT], F32, name="z_%d" % n)
             nc.vector.tensor_add(out=z[:], in0=z_sum[:], in1=bias[:])
-            value = late.tile([P, DOUT], F32, name="gate_%d" % n)
+            value = keep.tile([P, DOUT], F32, name="gate_%d" % n)
             nc.scalar.activation(out=value[:], in_=z[:], func=GATE_FUNC[n])
             gate.append(value)
 
             if n == GATE_F:
-                kept = late.tile([P, DOUT], F32)
+                kept = keep.tile([P, DOUT], F32)
                 nc.vector.tensor_mul(out=kept[:], in0=gate[GATE_F][:], in1=c_sb[:])
             if n == GATE_G:
-                fresh = late.tile([P, DOUT], F32)
+                fresh = keep.tile([P, DOUT], F32)
                 nc.vector.tensor_mul(out=fresh[:], in0=gate[GATE_I][:], in1=gate[GATE_G][:])
-                c_new = late.tile([P, DOUT], F32)
+                c_new = keep.tile([P, DOUT], F32)
                 nc.vector.tensor_add(out=c_new[:], in0=kept[:], in1=fresh[:])
-                tanh_c = late.tile([P, DOUT], F32)
+                tanh_c = keep.tile([P, DOUT], F32)
                 nc.scalar.activation(out=tanh_c[:], in_=c_new[:], func=ACT.Tanh)
                 nc.scalar.dma_start(out=out_1, in_=c_new[:])
             if n == GATE_O:
-                h_new = late.tile([P, DOUT], F32)
+                h_new = keep.tile([P, DOUT], F32)
                 nc.vector.tensor_mul(out=h_new[:], in0=gate[GATE_O][:], in1=tanh_c[:])
                 nc.sync.dma_start(out=out_0, in_=h_new[:])

@@ -14,18 +14,22 @@ ACT = mybir.ActivationFunctionType
 P = 128
 PACK = 4
 K_PASS = P * PACK
+BLOCK = 32
+BLOCK_PARTS = BLOCK // PACK
+PASS_BLOCKS = K_PASS // BLOCK
 DIN = 8192
 DOUT = 512
-X_PASSES = DIN // K_PASS
+CHUNK_PASSES = 4
+CHUNKS = DIN // (CHUNK_PASSES * K_PASS)
+X_PASSES = CHUNKS * CHUNK_PASSES
 H_PASS = X_PASSES
 PASSES = X_PASSES + 1
-CHUNK = 4
 BANK_PASSES = 2
 PAIRS = 2
 PASS_WORDS = K_PASS // 2
 QUADRANT = 32
-QUADRANT_ROWS = 4
-assert X_PASSES // CHUNK == QUADRANT_ROWS
+QUADRANTS = P // QUADRANT
+QUADRANT_ROWS = PASS_BLOCKS // QUADRANTS
 
 GATES = 4
 GATE_I, GATE_F, GATE_G, GATE_O = range(GATES)
@@ -52,17 +56,18 @@ def tile_lstmcell_k_kernel(
 
     with ExitStack() as ctx:
         keep = ctx.enter_context(tc.tile_pool(name="keep", bufs=1))
-        stage = ctx.enter_context(tc.tile_pool(name="stage", bufs=2))
         sums = ctx.enter_context(tc.psum_pool(name="sums", bufs=1))
         plain = ctx.enter_context(tc.psum_pool(name="plain", bufs=4))
 
-        xh = keep.tile([P, DIN + DOUT], BF16)
         c_sb = keep.tile([P, DOUT], BF16)
         w_words = [
             keep.tile([P, PASSES, DOUT], U32, align_bytes=64, name="w_words_%d" % n)
             for n in range(GATES)
         ]
-        wx_planes = keep.tile([P, X_PASSES, DOUT], U8, align_bytes=64)
+        wx_planes = [
+            keep.tile([P, CHUNK_PASSES, DOUT], U8, align_bytes=64, name="wx_planes_%d" % n)
+            for n in range(GATES)
+        ]
         wh_plane = [
             keep.tile([P, DOUT], U8, align_bytes=64, name="wh_plane_%d" % n)
             for n in range(GATES)
@@ -73,84 +78,106 @@ def tile_lstmcell_k_kernel(
         ones = keep.tile([P, P], BF16)
         bias_rows = keep.tile([P, GATES, DOUT], BF16)
 
-        nc.vector.memset(wx_planes[:].bitcast(I32), 0)
-        for n in range(GATES):
-            nc.vector.memset(wh_plane[n][:].bitcast(I32), 0)
         nc.vector.memset(bias_rows[:], 0.0)
         nc.vector.memset(ones[:], 1.0)
+        for n in range(GATES):
+            nc.vector.memset(wx_planes[n][:].bitcast(I32), 0)
+            nc.vector.memset(wh_plane[n][:].bitcast(I32), 0)
         masks.make_identity(nc, identity[:])
 
-        for n in range(GATES):
-            rows = wx_scales_in[n].rearrange("g (q r) n -> r q g n", r=QUADRANT_ROWS)
-            for r in range(QUADRANT_ROWS):
-                landing = wx_planes[QUADRANT_ROWS * n + r : P : QUADRANT, :, :]
-                if n < GATES // 2:
-                    nc.sync.dma_start(out=landing.bitcast(I32), in_=rows[r].bitcast(I32))
-                else:
-                    nc.gpsimd.dma_start(out=landing.bitcast(F32), in_=rows[r].bitcast(F32))
+        with tc.tile_pool(name="arrive", bufs=1) as arrive, tc.tile_pool(name="stage", bufs=2) as stage:
+            x_sb = arrive.tile([P, CHUNKS, PASS_BLOCKS, CHUNK_PASSES, BLOCK], BF16)
+            xh_passes = arrive.tile([P, PASSES, PASS_BLOCKS, BLOCK], BF16)
 
-        for first in range(0, X_PASSES, CHUNK):
-            cols = slice(first * K_PASS, (first + CHUNK) * K_PASS)
-            nc.sync.dma_start(out=xh[:, cols], in_=x[:, cols])
-        nc.sync.dma_start(out=xh[:, DIN:], in_=h)
-        nc.sync.dma_start(out=c_sb[:], in_=c)
-        for n in range(GATES):
-            nc.sync.dma_start(out=bias_rows[0:1, n, :], in_=bx_in[n].unsqueeze(0))
-            nc.sync.dma_start(out=bias_rows[1:2, n, :], in_=bh_in[n].unsqueeze(0))
-            wx_rows = wx_words_in[n].rearrange("g p n t -> p g (n t)")
-            wh_scale_rows = wh_scales_in[n].rearrange("g (q r) n -> r q (g n)", r=QUADRANT_ROWS)
-            for first in range(0, X_PASSES, CHUNK):
-                r = first // CHUNK
+            x_chunks = x.rearrange("b (j e) -> b j e", j=CHUNKS)
+            for j in range(CHUNKS):
                 nc.sync.dma_start(
-                    out=wh_plane[n][r:P:QUADRANT, :].bitcast(I32),
-                    in_=wh_scale_rows[r].bitcast(I32),
+                    out=x_sb[:, j].rearrange("b s c e -> b (s c e)"), in_=x_chunks[:, j, :]
                 )
-                nc.sync.dma_start(
-                    out=w_words[n][:, first : first + CHUNK, :].bitcast(I32),
-                    in_=wx_rows[:, first : first + CHUNK, :].bitcast(I32),
+            nc.sync.dma_start(out=xh_passes[:, H_PASS].rearrange("b s e -> b (s e)"), in_=h)
+            nc.sync.dma_start(out=c_sb[:], in_=c)
+            for n in range(GATES):
+                nc.sync.dma_start(out=bias_rows[0:1, n, :], in_=bx_in[n].unsqueeze(0))
+                nc.sync.dma_start(out=bias_rows[1:2, n, :], in_=bh_in[n].unsqueeze(0))
+                wx_blocks = (
+                    wx_words_in[n]
+                    .rearrange("g p n t -> (g p) (n t)")
+                    .rearrange(
+                        "(j s c i) b -> j c s i b",
+                        j=CHUNKS, s=PASS_BLOCKS, c=CHUNK_PASSES, i=BLOCK_PARTS,
+                    )
                 )
-            nc.sync.dma_start(
-                out=w_words[n][:, H_PASS, :].bitcast(I32),
-                in_=wh_words_in[n].rearrange("g p n t -> p (g n t)").bitcast(I32),
-            )
-
-        xh_pairs = xh[:].bitcast(F32)
-        banks_done = 0
-        for first in range(0, PASSES, CHUNK):
-            count = min(CHUNK, PASSES - first)
-            grouped = stage.tile([P, CHUNK, P, PACK], BF16, align_bytes=64)
-            for lead in range(0, count, BANK_PASSES):
-                here = min(BANK_PASSES, count - lead)
-                flipped = plain.tile([P, BANK_PASSES, PAIRS, P], F32, tag="plain")
-                for j in range(here):
-                    start = (first + lead + j) * PASS_WORDS
-                    for u in range(PAIRS):
-                        nc.tensor.transpose(
-                            flipped[:, j, u, :],
-                            xh_pairs[:, start + u : start + PASS_WORDS : PAIRS],
-                            identity[:],
+                for j in range(CHUNKS):
+                    for cc in range(CHUNK_PASSES):
+                        nc.sync.dma_start(
+                            out=w_words[n][:, j * CHUNK_PASSES + cc, :].bitcast(I32),
+                            in_=wx_blocks[j, cc].bitcast(I32),
                         )
-                copy_out = nc.vector.tensor_copy if banks_done % 2 == 0 else nc.scalar.copy
-                copy_out(
-                    out=grouped[:, lead : lead + here, :, :].bitcast(F32),
-                    in_=flipped[:, 0:here, :, :].rearrange("p j u b -> p j b u"),
+                nc.sync.dma_start(
+                    out=w_words[n][:, H_PASS, :].bitcast(I32),
+                    in_=wh_words_in[n].rearrange("g p n t -> p (g n t)").bitcast(I32),
                 )
-                banks_done += 1
-            nc.vector.quantize_mx(
-                out=xh_codes[:, first : first + count, :]
-                .rearrange("p g b -> p (g b)")
-                .bitcast(FP8X4),
-                scales=xh_planes[:, first : first + count, :].rearrange("p g b -> p (g b)"),
-                in_=grouped[:, 0:count, :, :].rearrange("p g b t -> p (g b t)"),
-            )
 
+            for n in range(GATES):
+                wx_rows = wx_scales_in[n].rearrange(
+                    "(j q) (r c) n -> q j r (c n)", q=QUADRANTS, c=CHUNK_PASSES
+                )
+                for q in range(QUADRANTS):
+                    nc.gpsimd.dma_start(
+                        out=wx_planes[n][q * QUADRANT : q * QUADRANT + PASS_BLOCKS, :, :]
+                        .rearrange("p c n -> p (c n)")
+                        .bitcast(F32),
+                        in_=wx_rows[q].bitcast(F32),
+                    )
+                wh_rows = wh_scales_in[n].rearrange("g (q r) n -> r q (g n)", r=QUADRANT_ROWS)
+                for r in range(QUADRANT_ROWS):
+                    nc.gpsimd.dma_start(
+                        out=wh_plane[n][r:P:QUADRANT, :].bitcast(F32), in_=wh_rows[r].bitcast(F32)
+                    )
+
+            xh_pairs = xh_passes[:].rearrange("b g s e -> b (g s e)").bitcast(F32)
+            banks_done = 0
+            for first in range(0, PASSES, CHUNK_PASSES):
+                count = min(CHUNK_PASSES, PASSES - first)
+                if first < X_PASSES:
+                    nc.vector.tensor_copy(
+                        out=xh_passes[:, first : first + count, :, :],
+                        in_=x_sb[:, first // CHUNK_PASSES].rearrange("b s c e -> b c s e"),
+                    )
+                grouped = stage.tile([P, CHUNK_PASSES, P, PACK], BF16, align_bytes=64)
+                for lead in range(0, count, BANK_PASSES):
+                    here = min(BANK_PASSES, count - lead)
+                    flipped = plain.tile([P, BANK_PASSES, PAIRS, P], F32, tag="plain")
+                    for j in range(here):
+                        start = (first + lead + j) * PASS_WORDS
+                        for u in range(PAIRS):
+                            nc.tensor.transpose(
+                                flipped[:, j, u, :],
+                                xh_pairs[:, start + u : start + PASS_WORDS : PAIRS],
+                                identity[:],
+                            )
+                    copy_out = nc.vector.tensor_copy if banks_done % 2 == 0 else nc.scalar.copy
+                    copy_out(
+                        out=grouped[:, lead : lead + here, :, :].bitcast(F32),
+                        in_=flipped[:, 0:here, :, :].rearrange("p j u b -> p j b u"),
+                    )
+                    banks_done += 1
+                nc.vector.quantize_mx(
+                    out=xh_codes[:, first : first + count, :]
+                    .rearrange("p g b -> p (g b)")
+                    .bitcast(FP8X4),
+                    scales=xh_planes[:, first : first + count, :].rearrange("p g b -> p (g b)"),
+                    in_=grouped[:, 0:count, :, :].rearrange("p g b t -> p (g b t)"),
+                )
+
+        late = ctx.enter_context(tc.tile_pool(name="late", bufs=1))
         gate = []
         for n in range(GATES):
             spread = plain.tile([P, DOUT], F32, tag="plain")
             nc.tensor.matmul(
                 out=spread[:], lhsT=ones[:], rhs=bias_rows[:, n, :], start=True, stop=True
             )
-            bias = keep.tile([P, DOUT], F32, name="bias_%d" % n)
+            bias = late.tile([P, DOUT], F32, name="bias_%d" % n)
             nc.scalar.copy(out=bias[:], in_=spread[:])
 
             z_sum = sums.tile([P, DOUT], F32, name="z_sum_%d" % n)
@@ -158,7 +185,9 @@ def tile_lstmcell_k_kernel(
                 if g == H_PASS:
                     w_plane = wh_plane[n][:]
                 else:
-                    w_plane = wx_planes[QUADRANT_ROWS * n : P, g, :]
+                    w_plane = wx_planes[n][
+                        QUADRANT_ROWS * (g // CHUNK_PASSES) : P, g % CHUNK_PASSES, :
+                    ]
                 nc.tensor.matmul_mx(
                     out=z_sum[:],
                     lhsT=xh_codes[:, g, :].bitcast(FP8X4),
@@ -168,24 +197,24 @@ def tile_lstmcell_k_kernel(
                     start=(g == 0),
                     stop=(g == PASSES - 1),
                 )
-            z = keep.tile([P, DOUT], F32, name="z_%d" % n)
+            z = late.tile([P, DOUT], F32, name="z_%d" % n)
             nc.vector.tensor_add(out=z[:], in0=z_sum[:], in1=bias[:])
-            value = keep.tile([P, DOUT], F32, name="gate_%d" % n)
+            value = late.tile([P, DOUT], F32, name="gate_%d" % n)
             nc.scalar.activation(out=value[:], in_=z[:], func=GATE_FUNC[n])
             gate.append(value)
 
             if n == GATE_F:
-                kept = keep.tile([P, DOUT], F32)
+                kept = late.tile([P, DOUT], F32)
                 nc.vector.tensor_mul(out=kept[:], in0=gate[GATE_F][:], in1=c_sb[:])
             if n == GATE_G:
-                fresh = keep.tile([P, DOUT], F32)
+                fresh = late.tile([P, DOUT], F32)
                 nc.vector.tensor_mul(out=fresh[:], in0=gate[GATE_I][:], in1=gate[GATE_G][:])
-                c_new = keep.tile([P, DOUT], F32)
+                c_new = late.tile([P, DOUT], F32)
                 nc.vector.tensor_add(out=c_new[:], in0=kept[:], in1=fresh[:])
-                tanh_c = keep.tile([P, DOUT], F32)
+                tanh_c = late.tile([P, DOUT], F32)
                 nc.scalar.activation(out=tanh_c[:], in_=c_new[:], func=ACT.Tanh)
                 nc.scalar.dma_start(out=out_1, in_=c_new[:])
             if n == GATE_O:
-                h_new = keep.tile([P, DOUT], F32)
+                h_new = late.tile([P, DOUT], F32)
                 nc.vector.tensor_mul(out=h_new[:], in0=gate[GATE_O][:], in1=tanh_c[:])
                 nc.sync.dma_start(out=out_0, in_=h_new[:])

@@ -14,22 +14,18 @@ ACT = mybir.ActivationFunctionType
 P = 128
 PACK = 4
 K_PASS = P * PACK
-BLOCK = 32
-BLOCK_PARTS = BLOCK // PACK
-PASS_BLOCKS = K_PASS // BLOCK
 DIN = 8192
 DOUT = 512
-CHUNK_PASSES = 4
-CHUNKS = DIN // (CHUNK_PASSES * K_PASS)
-X_PASSES = CHUNKS * CHUNK_PASSES
+X_PASSES = DIN // K_PASS
 H_PASS = X_PASSES
 PASSES = X_PASSES + 1
+CHUNK = 4
 BANK_PASSES = 2
 PAIRS = 2
 PASS_WORDS = K_PASS // 2
 QUADRANT = 32
-QUADRANTS = P // QUADRANT
-QUADRANT_ROWS = PASS_BLOCKS // QUADRANTS
+QUADRANT_ROWS = 4
+assert X_PASSES // CHUNK == QUADRANT_ROWS
 
 GATES = 4
 GATE_I, GATE_F, GATE_G, GATE_O = range(GATES)
@@ -56,18 +52,17 @@ def tile_lstmcell_k_kernel(
 
     with ExitStack() as ctx:
         keep = ctx.enter_context(tc.tile_pool(name="keep", bufs=1))
+        stage = ctx.enter_context(tc.tile_pool(name="stage", bufs=2))
         sums = ctx.enter_context(tc.psum_pool(name="sums", bufs=1))
         plain = ctx.enter_context(tc.psum_pool(name="plain", bufs=4))
 
+        xh = keep.tile([P, DIN + DOUT], BF16)
         c_sb = keep.tile([P, DOUT], BF16)
         w_words = [
             keep.tile([P, PASSES, DOUT], U32, align_bytes=64, name="w_words_%d" % n)
             for n in range(GATES)
         ]
-        wx_planes = [
-            keep.tile([P, CHUNK_PASSES, DOUT], U8, align_bytes=64, name="wx_planes_%d" % n)
-            for n in range(GATES)
-        ]
+        wx_planes = keep.tile([P, X_PASSES, DOUT], U8, align_bytes=64)
         wh_plane = [
             keep.tile([P, DOUT], U8, align_bytes=64, name="wh_plane_%d" % n)
             for n in range(GATES)
@@ -78,106 +73,85 @@ def tile_lstmcell_k_kernel(
         ones = keep.tile([P, P], BF16)
         bias_rows = keep.tile([P, GATES, DOUT], BF16)
 
+        nc.vector.memset(wx_planes[:].bitcast(I32), 0)
+        for n in range(GATES):
+            nc.vector.memset(wh_plane[n][:].bitcast(I32), 0)
         nc.vector.memset(bias_rows[:], 0.0)
         nc.vector.memset(ones[:], 1.0)
-        for n in range(GATES):
-            nc.vector.memset(wx_planes[n][:].bitcast(I32), 0)
-            nc.vector.memset(wh_plane[n][:].bitcast(I32), 0)
         masks.make_identity(nc, identity[:])
 
-        with tc.tile_pool(name="arrive", bufs=1) as arrive, tc.tile_pool(name="stage", bufs=2) as stage:
-            x_sb = arrive.tile([P, CHUNKS, PASS_BLOCKS, CHUNK_PASSES, BLOCK], BF16)
-            xh_passes = arrive.tile([P, PASSES, PASS_BLOCKS, BLOCK], BF16)
+        for first in range(0, X_PASSES, CHUNK):
+            cols = slice(first * K_PASS, (first + CHUNK) * K_PASS)
+            nc.sync.dma_start(out=xh[:, cols], in_=x[:, cols])
+        nc.sync.dma_start(out=xh[:, DIN:], in_=h)
+        nc.sync.dma_start(out=c_sb[:], in_=c)
 
-            x_chunks = x.rearrange("b (j e) -> b j e", j=CHUNKS)
-            for j in range(CHUNKS):
+        for n in range(GATES):
+            rows = wx_scales_in[n].rearrange("g (q r) n -> r q g n", r=QUADRANT_ROWS)
+            for r in range(QUADRANT_ROWS):
+                landing = wx_planes[QUADRANT_ROWS * n + r : P : QUADRANT, :, :]
+                if n < GATES // 2:
+                    nc.sync.dma_start(out=landing.bitcast(I32), in_=rows[r].bitcast(I32))
+                else:
+                    nc.gpsimd.dma_start(out=landing.bitcast(F32), in_=rows[r].bitcast(F32))
+
+        for n in range(GATES):
+            nc.sync.dma_start(out=bias_rows[0:1, n, :], in_=bx_in[n].unsqueeze(0))
+            nc.sync.dma_start(out=bias_rows[1:2, n, :], in_=bh_in[n].unsqueeze(0))
+            wx_rows = wx_words_in[n].rearrange("g p n t -> p g (n t)")
+            wh_scale_rows = wh_scales_in[n].rearrange("g (q r) n -> r q (g n)", r=QUADRANT_ROWS)
+            for first in range(0, X_PASSES, CHUNK):
+                r = first // CHUNK
                 nc.sync.dma_start(
-                    out=x_sb[:, j].rearrange("b s c e -> b (s c e)"), in_=x_chunks[:, j, :]
+                    out=wh_plane[n][r:P:QUADRANT, :].bitcast(I32),
+                    in_=wh_scale_rows[r].bitcast(I32),
                 )
-            nc.sync.dma_start(out=xh_passes[:, H_PASS].rearrange("b s e -> b (s e)"), in_=h)
-            nc.sync.dma_start(out=c_sb[:], in_=c)
-            for n in range(GATES):
-                nc.sync.dma_start(out=bias_rows[0:1, n, :], in_=bx_in[n].unsqueeze(0))
-                nc.sync.dma_start(out=bias_rows[1:2, n, :], in_=bh_in[n].unsqueeze(0))
-                wx_blocks = (
-                    wx_words_in[n]
-                    .rearrange("g p n t -> (g p) (n t)")
-                    .rearrange(
-                        "(j s c i) b -> j c s i b",
-                        j=CHUNKS, s=PASS_BLOCKS, c=CHUNK_PASSES, i=BLOCK_PARTS,
-                    )
+                nc.sync.dma_start(
+                    out=w_words[n][:, first : first + CHUNK, :].bitcast(I32),
+                    in_=wx_rows[:, first : first + CHUNK, :].bitcast(I32),
                 )
-                for j in range(CHUNKS):
-                    for cc in range(CHUNK_PASSES):
-                        nc.sync.dma_start(
-                            out=w_words[n][:, j * CHUNK_PASSES + cc, :].bitcast(I32),
-                            in_=wx_blocks[j, cc].bitcast(I32),
+            nc.sync.dma_start(
+                out=w_words[n][:, H_PASS, :].bitcast(I32),
+                in_=wh_words_in[n].rearrange("g p n t -> p (g n t)").bitcast(I32),
+            )
+
+        xh_pairs = xh[:].bitcast(F32)
+        banks_done = 0
+        for first in range(0, PASSES, CHUNK):
+            count = min(CHUNK, PASSES - first)
+            grouped = stage.tile([P, CHUNK, P, PACK], BF16, align_bytes=64)
+            for lead in range(0, count, BANK_PASSES):
+                here = min(BANK_PASSES, count - lead)
+                flipped = plain.tile([P, BANK_PASSES, PAIRS, P], F32, tag="plain")
+                for j in range(here):
+                    start = (first + lead + j) * PASS_WORDS
+                    for u in range(PAIRS):
+                        nc.tensor.transpose(
+                            flipped[:, j, u, :],
+                            xh_pairs[:, start + u : start + PASS_WORDS : PAIRS],
+                            identity[:],
                         )
-                nc.sync.dma_start(
-                    out=w_words[n][:, H_PASS, :].bitcast(I32),
-                    in_=wh_words_in[n].rearrange("g p n t -> p (g n t)").bitcast(I32),
+                copy_out = nc.vector.tensor_copy if banks_done % 2 == 0 else nc.scalar.copy
+                copy_out(
+                    out=grouped[:, lead : lead + here, :, :].bitcast(F32),
+                    in_=flipped[:, 0:here, :, :].rearrange("p j u b -> p j b u"),
                 )
+                banks_done += 1
+            nc.vector.quantize_mx(
+                out=xh_codes[:, first : first + count, :]
+                .rearrange("p g b -> p (g b)")
+                .bitcast(FP8X4),
+                scales=xh_planes[:, first : first + count, :].rearrange("p g b -> p (g b)"),
+                in_=grouped[:, 0:count, :, :].rearrange("p g b t -> p (g b t)"),
+            )
 
-            for n in range(GATES):
-                wx_rows = wx_scales_in[n].rearrange(
-                    "(j q) (r c) n -> q j r (c n)", q=QUADRANTS, c=CHUNK_PASSES
-                )
-                for q in range(QUADRANTS):
-                    nc.gpsimd.dma_start(
-                        out=wx_planes[n][q * QUADRANT : q * QUADRANT + PASS_BLOCKS, :, :]
-                        .rearrange("p c n -> p (c n)")
-                        .bitcast(F32),
-                        in_=wx_rows[q].bitcast(F32),
-                    )
-                wh_rows = wh_scales_in[n].rearrange("g (q r) n -> r q (g n)", r=QUADRANT_ROWS)
-                for r in range(QUADRANT_ROWS):
-                    nc.gpsimd.dma_start(
-                        out=wh_plane[n][r:P:QUADRANT, :].bitcast(F32), in_=wh_rows[r].bitcast(F32)
-                    )
-
-            xh_pairs = xh_passes[:].rearrange("b g s e -> b (g s e)").bitcast(F32)
-            banks_done = 0
-            for first in range(0, PASSES, CHUNK_PASSES):
-                count = min(CHUNK_PASSES, PASSES - first)
-                if first < X_PASSES:
-                    nc.vector.tensor_copy(
-                        out=xh_passes[:, first : first + count, :, :],
-                        in_=x_sb[:, first // CHUNK_PASSES].rearrange("b s c e -> b c s e"),
-                    )
-                grouped = stage.tile([P, CHUNK_PASSES, P, PACK], BF16, align_bytes=64)
-                for lead in range(0, count, BANK_PASSES):
-                    here = min(BANK_PASSES, count - lead)
-                    flipped = plain.tile([P, BANK_PASSES, PAIRS, P], F32, tag="plain")
-                    for j in range(here):
-                        start = (first + lead + j) * PASS_WORDS
-                        for u in range(PAIRS):
-                            nc.tensor.transpose(
-                                flipped[:, j, u, :],
-                                xh_pairs[:, start + u : start + PASS_WORDS : PAIRS],
-                                identity[:],
-                            )
-                    copy_out = nc.vector.tensor_copy if banks_done % 2 == 0 else nc.scalar.copy
-                    copy_out(
-                        out=grouped[:, lead : lead + here, :, :].bitcast(F32),
-                        in_=flipped[:, 0:here, :, :].rearrange("p j u b -> p j b u"),
-                    )
-                    banks_done += 1
-                nc.vector.quantize_mx(
-                    out=xh_codes[:, first : first + count, :]
-                    .rearrange("p g b -> p (g b)")
-                    .bitcast(FP8X4),
-                    scales=xh_planes[:, first : first + count, :].rearrange("p g b -> p (g b)"),
-                    in_=grouped[:, 0:count, :, :].rearrange("p g b t -> p (g b t)"),
-                )
-
-        late = ctx.enter_context(tc.tile_pool(name="late", bufs=1))
         gate = []
         for n in range(GATES):
             spread = plain.tile([P, DOUT], F32, tag="plain")
             nc.tensor.matmul(
                 out=spread[:], lhsT=ones[:], rhs=bias_rows[:, n, :], start=True, stop=True
             )
-            bias = late.tile([P, DOUT], F32, name="bias_%d" % n)
+            bias = keep.tile([P, DOUT], F32, name="bias_%d" % n)
             nc.scalar.copy(out=bias[:], in_=spread[:])
 
             z_sum = sums.tile([P, DOUT], F32, name="z_sum_%d" % n)
@@ -185,9 +159,7 @@ def tile_lstmcell_k_kernel(
                 if g == H_PASS:
                     w_plane = wh_plane[n][:]
                 else:
-                    w_plane = wx_planes[n][
-                        QUADRANT_ROWS * (g // CHUNK_PASSES) : P, g % CHUNK_PASSES, :
-                    ]
+                    w_plane = wx_planes[QUADRANT_ROWS * n : P, g, :]
                 nc.tensor.matmul_mx(
                     out=z_sum[:],
                     lhsT=xh_codes[:, g, :].bitcast(FP8X4),
@@ -197,24 +169,24 @@ def tile_lstmcell_k_kernel(
                     start=(g == 0),
                     stop=(g == PASSES - 1),
                 )
-            z = late.tile([P, DOUT], F32, name="z_%d" % n)
+            z = keep.tile([P, DOUT], F32, name="z_%d" % n)
             nc.vector.tensor_add(out=z[:], in0=z_sum[:], in1=bias[:])
-            value = late.tile([P, DOUT], F32, name="gate_%d" % n)
+            value = keep.tile([P, DOUT], F32, name="gate_%d" % n)
             nc.scalar.activation(out=value[:], in_=z[:], func=GATE_FUNC[n])
             gate.append(value)
 
             if n == GATE_F:
-                kept = late.tile([P, DOUT], F32)
+                kept = keep.tile([P, DOUT], F32)
                 nc.vector.tensor_mul(out=kept[:], in0=gate[GATE_F][:], in1=c_sb[:])
             if n == GATE_G:
-                fresh = late.tile([P, DOUT], F32)
+                fresh = keep.tile([P, DOUT], F32)
                 nc.vector.tensor_mul(out=fresh[:], in0=gate[GATE_I][:], in1=gate[GATE_G][:])
-                c_new = late.tile([P, DOUT], F32)
+                c_new = keep.tile([P, DOUT], F32)
                 nc.vector.tensor_add(out=c_new[:], in0=kept[:], in1=fresh[:])
-                tanh_c = late.tile([P, DOUT], F32)
+                tanh_c = keep.tile([P, DOUT], F32)
                 nc.scalar.activation(out=tanh_c[:], in_=c_new[:], func=ACT.Tanh)
                 nc.scalar.dma_start(out=out_1, in_=c_new[:])
             if n == GATE_O:
-                h_new = late.tile([P, DOUT], F32)
+                h_new = keep.tile([P, DOUT], F32)
                 nc.vector.tensor_mul(out=h_new[:], in0=gate[GATE_O][:], in1=tanh_c[:])
                 nc.sync.dma_start(out=out_0, in_=h_new[:])

@@ -86,11 +86,11 @@ def tile_lstmcell_k_kernel(
         nc.sync.dma_start(out=xh[:, DIN:], in_=h)
         nc.sync.dma_start(out=c_sb[:], in_=c)
 
-        for n in range(GATES):
-            rows = wx_scales_in[n].rearrange("g (q r) n -> r q g n", r=QUADRANT_ROWS)
-            for r in range(QUADRANT_ROWS):
+        for r in range(QUADRANT_ROWS):
+            for n in range(GATES):
+                rows = wx_scales_in[n].rearrange("g (q r) n -> r q g n", r=QUADRANT_ROWS)
                 landing = wx_planes[QUADRANT_ROWS * n + r : P : QUADRANT, :, :]
-                if n < GATES // 2:
+                if n != GATE_O:
                     nc.sync.dma_start(out=landing.bitcast(I32), in_=rows[r].bitcast(I32))
                 else:
                     nc.gpsimd.dma_start(out=landing.bitcast(F32), in_=rows[r].bitcast(F32))

@@ -90,10 +90,7 @@ def tile_lstmcell_k_kernel(
             for n in range(GATES):
                 rows = wx_scales_in[n].rearrange("g (q r) n -> r q g n", r=QUADRANT_ROWS)
                 landing = wx_planes[QUADRANT_ROWS * n + r : P : QUADRANT, :, :]
-                if n != GATE_O:
-                    nc.sync.dma_start(out=landing.bitcast(I32), in_=rows[r].bitcast(I32))
-                else:
-                    nc.gpsimd.dma_start(out=landing.bitcast(F32), in_=rows[r].bitcast(F32))
+                nc.sync.dma_start(out=landing.bitcast(I32), in_=rows[r].bitcast(I32))
 
         for n in range(GATES):
             nc.sync.dma_start(out=bias_rows[0:1, n, :], in_=bx_in[n].unsqueeze(0))

@@ -27,6 +27,10 @@ QUADRANT = 32
 QUADRANT_ROWS = 4
 assert X_PASSES // CHUNK == QUADRANT_ROWS
 
+LATE_FIRST = 12
+LATE_PIECES = ((12, 2), (14, 1), (15, 1))
+HALF = 256
+
 GATES = 4
 GATE_I, GATE_F, GATE_G, GATE_O = range(GATES)
 GATE_FUNC = (ACT.Sigmoid, ACT.Sigmoid, ACT.Tanh, ACT.Sigmoid)
@@ -92,25 +96,42 @@ def tile_lstmcell_k_kernel(
                 landing = wx_planes[QUADRANT_ROWS * n + r : P : QUADRANT, :, :]
                 nc.sync.dma_start(out=landing.bitcast(I32), in_=rows[r].bitcast(I32))
 
-        for n in range(GATES):
-            nc.sync.dma_start(out=bias_rows[0:1, n, :], in_=bx_in[n].unsqueeze(0))
-            nc.sync.dma_start(out=bias_rows[1:2, n, :], in_=bh_in[n].unsqueeze(0))
+        def load_wx(n, first, count):
             wx_rows = wx_words_in[n].rearrange("g p n t -> p g (n t)")
-            wh_scale_rows = wh_scales_in[n].rearrange("g (q r) n -> r q (g n)", r=QUADRANT_ROWS)
-            for first in range(0, X_PASSES, CHUNK):
-                r = first // CHUNK
-                nc.sync.dma_start(
-                    out=wh_plane[n][r:P:QUADRANT, :].bitcast(I32),
-                    in_=wh_scale_rows[r].bitcast(I32),
-                )
-                nc.sync.dma_start(
-                    out=w_words[n][:, first : first + CHUNK, :].bitcast(I32),
-                    in_=wx_rows[:, first : first + CHUNK, :].bitcast(I32),
-                )
+            nc.sync.dma_start(
+                out=w_words[n][:, first : first + count, :].bitcast(I32),
+                in_=wx_rows[:, first : first + count, :].bitcast(I32),
+            )
+
+        def load_wh(n):
             nc.sync.dma_start(
                 out=w_words[n][:, H_PASS, :].bitcast(I32),
                 in_=wh_words_in[n].rearrange("g p n t -> p (g n t)").bitcast(I32),
             )
+
+        def load_wh_scale(n, r):
+            wh_scale_rows = wh_scales_in[n].rearrange("g (q r) n -> r q (g n)", r=QUADRANT_ROWS)
+            nc.sync.dma_start(
+                out=wh_plane[n][r:P:QUADRANT, :].bitcast(I32),
+                in_=wh_scale_rows[r].bitcast(I32),
+            )
+
+        for n in range(GATES):
+            nc.sync.dma_start(out=bias_rows[0:1, n, :], in_=bx_in[n].unsqueeze(0))
+            nc.sync.dma_start(out=bias_rows[1:2, n, :], in_=bh_in[n].unsqueeze(0))
+            if n != GATE_O:
+                for r in range(QUADRANT_ROWS):
+                    load_wh_scale(n, r)
+                    load_wx(n, r * CHUNK, CHUNK)
+                load_wh(n)
+            else:
+                for r in range(QUADRANT_ROWS - 1):
+                    load_wh_scale(n, r)
+                    load_wx(n, r * CHUNK, CHUNK)
+                load_wh_scale(n, QUADRANT_ROWS - 1)
+                load_wh(n)
+                for first, count in LATE_PIECES:
+                    load_wx(n, first, count)
 
         xh_pairs = xh[:].bitcast(F32)
         banks_done = 0
@@ -151,25 +172,33 @@ def tile_lstmcell_k_kernel(
             bias = keep.tile([P, DOUT], F32, name="bias_%d" % n)
             nc.scalar.copy(out=bias[:], in_=spread[:])
 
-            z_sum = sums.tile([P, DOUT], F32, name="z_sum_%d" % n)
-            for g in range(PASSES):
+            def mx_pass(out, g, cols, start, stop):
                 if g == H_PASS:
-                    w_plane = wh_plane[n][:]
+                    w_plane = wh_plane[n][:, cols]
                 else:
-                    w_plane = wx_planes[QUADRANT_ROWS * n : P, g, :]
+                    w_plane = wx_planes[QUADRANT_ROWS * n : P, g, cols]
                 nc.tensor.matmul_mx(
-                    out=z_sum[:],
+                    out=out,
                     lhsT=xh_codes[:, g, :].bitcast(FP8X4),
                     lhsT_scale=xh_planes[:, g, :],
-                    rhs=w_words[n][:, g, :].bitcast(FP8X4),
+                    rhs=w_words[n][:, g, cols].bitcast(FP8X4),
                     rhs_scale=w_plane,
-                    start=(g == 0),
-                    stop=(g == PASSES - 1),
+                    start=start,
+                    stop=stop,
                 )
+
+            z_sum = sums.tile([P, DOUT], F32, name="z_sum_%d" % n, tag="bank_%d" % n)
+            if n == GATE_O:
+                group = list(range(LATE_FIRST)) + [H_PASS]
+            else:
+                group = list(range(PASSES))
+            for g in group:
+                mx_pass(z_sum[:], g, slice(0, DOUT), g == group[0], g == group[-1])
             z = keep.tile([P, DOUT], F32, name="z_%d" % n)
             nc.vector.tensor_add(out=z[:], in0=z_sum[:], in1=bias[:])
             value = keep.tile([P, DOUT], F32, name="gate_%d" % n)
-            nc.scalar.activation(out=value[:], in_=z[:], func=GATE_FUNC[n])
+            if n != GATE_O:
+                nc.scalar.activation(out=value[:], in_=z[:], func=GATE_FUNC[n])
             gate.append(value)
 
             if n == GATE_F:
@@ -184,6 +213,23 @@ def tile_lstmcell_k_kernel(
                 nc.scalar.activation(out=tanh_c[:], in_=c_new[:], func=ACT.Tanh)
                 nc.scalar.dma_start(out=out_1, in_=c_new[:])
             if n == GATE_O:
+                halves = [slice(j * HALF, (j + 1) * HALF) for j in range(DOUT // HALF)]
+                late = [
+                    sums.tile([P, HALF], F32, name="late_%d" % j, tag="bank_%d" % j)
+                    for j in range(len(halves))
+                ]
+                for g in range(LATE_FIRST, X_PASSES):
+                    for j, cols in enumerate(halves):
+                        mx_pass(late[j][:], g, cols, g == LATE_FIRST, g == X_PASSES - 1)
+                z_whole = keep.tile([P, DOUT], F32)
                 h_new = keep.tile([P, DOUT], F32)
-                nc.vector.tensor_mul(out=h_new[:], in0=gate[GATE_O][:], in1=tanh_c[:])
-                nc.sync.dma_start(out=out_0, in_=h_new[:])
+                for j, cols in enumerate(halves):
+                    nc.vector.tensor_add(out=z_whole[:, cols], in0=late[j][:], in1=z[:, cols])
+                    nc.scalar.activation(
+                        out=value[:, cols], in_=z_whole[:, cols], func=GATE_FUNC[n]
+                    )
+                for cols in halves:
+                    nc.vector.tensor_mul(
+                        out=h_new[:, cols], in0=value[:, cols], in1=tanh_c[:, cols]
+                    )
+                    nc.sync.dma_start(out=out_0[:, cols], in_=h_new[:, cols])

@@ -19,6 +19,7 @@ DOUT = 512
 X_PASSES = DIN // K_PASS
 H_PASS = X_PASSES
 PASSES = X_PASSES + 1
+BIG_CHUNK = 8
 CHUNK = 4
 BANK_PASSES = 2
 PAIRS = 2
@@ -55,6 +56,7 @@ def tile_lstmcell_k_kernel(
     bh_in = (bhi, bhf, bhg, bho)
 
     with ExitStack() as ctx:
+        ctx.enter_context(tc.manual_schedule(engines=set([mybir.EngineType.SP])))
         keep = ctx.enter_context(tc.tile_pool(name="keep", bufs=1))
         stage = ctx.enter_context(tc.tile_pool(name="stage", bufs=2))
         sums = ctx.enter_context(tc.psum_pool(name="sums", bufs=1))
@@ -84,8 +86,8 @@ def tile_lstmcell_k_kernel(
         nc.vector.memset(ones[:], 1.0)
         masks.make_identity(nc, identity[:])
 
-        for first in range(0, X_PASSES, CHUNK):
-            cols = slice(first * K_PASS, (first + CHUNK) * K_PASS)
+        for first in range(0, X_PASSES, BIG_CHUNK):
+            cols = slice(first * K_PASS, (first + BIG_CHUNK) * K_PASS)
             nc.sync.dma_start(out=xh[:, cols], in_=x[:, cols])
         nc.sync.dma_start(out=xh[:, DIN:], in_=h)
         nc.sync.dma_start(out=c_sb[:], in_=c)
@@ -117,14 +119,19 @@ def tile_lstmcell_k_kernel(
             )
 
         for n in range(GATES):
-            nc.sync.dma_start(out=bias_rows[0:1, n, :], in_=bx_in[n].unsqueeze(0))
-            nc.sync.dma_start(out=bias_rows[1:2, n, :], in_=bh_in[n].unsqueeze(0))
             if n != GATE_O:
-                for r in range(QUADRANT_ROWS):
-                    load_wh_scale(n, r)
-                    load_wx(n, r * CHUNK, CHUNK)
+                nc.sync.dma_start(out=bias_rows[0:1, n, :], in_=bx_in[n].unsqueeze(0))
+                nc.sync.dma_start(out=bias_rows[1:2, n, :], in_=bh_in[n].unsqueeze(0))
+                load_wh_scale(n, 0)
+                load_wx(n, 0, BIG_CHUNK)
+                load_wh_scale(n, 1)
+                load_wh_scale(n, 2)
+                load_wx(n, BIG_CHUNK, BIG_CHUNK)
+                load_wh_scale(n, 3)
                 load_wh(n)
             else:
+                nc.sync.dma_start(out=bias_rows[0:1, n, :], in_=bx_in[n].unsqueeze(0))
+                nc.sync.dma_start(out=bias_rows[1:2, n, :], in_=bh_in[n].unsqueeze(0))
                 for r in range(QUADRANT_ROWS - 1):
                     load_wh_scale(n, r)
                     load_wx(n, r * CHUNK, CHUNK)
@@ -211,7 +218,7 @@ def tile_lstmcell_k_kernel(
                 nc.vector.tensor_add(out=c_new[:], in0=kept[:], in1=fresh[:])
                 tanh_c = keep.tile([P, DOUT], F32)
                 nc.scalar.activation(out=tanh_c[:], in_=c_new[:], func=ACT.Tanh)
-                nc.scalar.dma_start(out=out_1, in_=c_new[:])
+                nc.sync.dma_start(out=out_1, in_=c_new[:])
             if n == GATE_O:
                 halves = [slice(j * HALF, (j + 1) * HALF) for j in range(DOUT // HALF)]
                 late = [

from contextlib import ExitStack

import concourse.masks as masks
import concourse.mybir as mybir

F32 = mybir.dt.float32
BF16 = mybir.dt.bfloat16
I32 = mybir.dt.int32
U32 = mybir.dt.uint32
U8 = mybir.dt.uint8
FP8X4 = mybir.dt.float8_e4m3fn_x4
ACT = mybir.ActivationFunctionType

P = 128
PACK = 4
K_PASS = P * PACK
DIN = 8192
DOUT = 512
X_PASSES = DIN // K_PASS
H_PASS = X_PASSES
PASSES = X_PASSES + 1
BIG_CHUNK = 8
CHUNK = 4
BANK_PASSES = 2
PAIRS = 2
PASS_WORDS = K_PASS // 2
QUADRANT = 32
QUADRANT_ROWS = 4
assert X_PASSES // CHUNK == QUADRANT_ROWS

LATE_FIRST = 12
LATE_PIECES = ((12, 2), (14, 1), (15, 1))
HALF = 256

GATES = 4
GATE_I, GATE_F, GATE_G, GATE_O = range(GATES)
GATE_FUNC = (ACT.Sigmoid, ACT.Sigmoid, ACT.Tanh, ACT.Sigmoid)

FLOPS = 2 * P * (DIN + DOUT) * GATES * DOUT


def tile_lstmcell_k_kernel(
    tc, x, h, c,
    Wxi_words, Wxi_scales, Whi_words, Whi_scales, bxi, bhi,
    Wxf_words, Wxf_scales, Whf_words, Whf_scales, bxf, bhf,
    Wxg_words, Wxg_scales, Whg_words, Whg_scales, bxg, bhg,
    Wxo_words, Wxo_scales, Who_words, Who_scales, bxo, bho,
    out_0, out_1,
):
    nc = tc.nc
    wx_words_in = (Wxi_words, Wxf_words, Wxg_words, Wxo_words)
    wx_scales_in = (Wxi_scales, Wxf_scales, Wxg_scales, Wxo_scales)
    wh_words_in = (Whi_words, Whf_words, Whg_words, Who_words)
    wh_scales_in = (Whi_scales, Whf_scales, Whg_scales, Who_scales)
    bx_in = (bxi, bxf, bxg, bxo)
    bh_in = (bhi, bhf, bhg, bho)

    with ExitStack() as ctx:
        ctx.enter_context(tc.manual_schedule(engines=set([mybir.EngineType.SP])))
        keep = ctx.enter_context(tc.tile_pool(name="keep", bufs=1))
        stage = ctx.enter_context(tc.tile_pool(name="stage", bufs=2))
        sums = ctx.enter_context(tc.psum_pool(name="sums", bufs=1))
        plain = ctx.enter_context(tc.psum_pool(name="plain", bufs=4))

        xh = keep.tile([P, DIN + DOUT], BF16)
        c_sb = keep.tile([P, DOUT], BF16)
        w_words = [
            keep.tile([P, PASSES, DOUT], U32, align_bytes=64, name="w_words_%d" % n)
            for n in range(GATES)
        ]
        wx_planes = keep.tile([P, X_PASSES, DOUT], U8, align_bytes=64)
        wh_plane = [
            keep.tile([P, DOUT], U8, align_bytes=64, name="wh_plane_%d" % n)
            for n in range(GATES)
        ]
        xh_codes = keep.tile([P, PASSES, P], U32, align_bytes=64)
        xh_planes = keep.tile([P, PASSES, P], U8, align_bytes=64)
        identity = keep.tile([P, P], F32)
        ones = keep.tile([P, P], BF16)
        bias_rows = keep.tile([P, GATES, DOUT], BF16)

        nc.vector.memset(wx_planes[:].bitcast(I32), 0)
        for n in range(GATES):
            nc.vector.memset(wh_plane[n][:].bitcast(I32), 0)
        nc.vector.memset(bias_rows[:], 0.0)
        nc.vector.memset(ones[:], 1.0)
        masks.make_identity(nc, identity[:])

        for first in range(0, X_PASSES, BIG_CHUNK):
            cols = slice(first * K_PASS, (first + BIG_CHUNK) * K_PASS)
            nc.sync.dma_start(out=xh[:, cols], in_=x[:, cols])
        nc.sync.dma_start(out=xh[:, DIN:], in_=h)
        nc.sync.dma_start(out=c_sb[:], in_=c)

        for r in range(QUADRANT_ROWS):
            for n in range(GATES):
                rows = wx_scales_in[n].rearrange("g (q r) n -> r q g n", r=QUADRANT_ROWS)
                landing = wx_planes[QUADRANT_ROWS * n + r : P : QUADRANT, :, :]
                nc.sync.dma_start(out=landing.bitcast(I32), in_=rows[r].bitcast(I32))

        def load_wx(n, first, count):
            wx_rows = wx_words_in[n].rearrange("g p n t -> p g (n t)")
            nc.sync.dma_start(
                out=w_words[n][:, first : first + count, :].bitcast(I32),
                in_=wx_rows[:, first : first + count, :].bitcast(I32),
            )

        def load_wh(n):
            nc.sync.dma_start(
                out=w_words[n][:, H_PASS, :].bitcast(I32),
                in_=wh_words_in[n].rearrange("g p n t -> p (g n t)").bitcast(I32),
            )

        def load_wh_scale(n, r):
            wh_scale_rows = wh_scales_in[n].rearrange("g (q r) n -> r q (g n)", r=QUADRANT_ROWS)
            nc.sync.dma_start(
                out=wh_plane[n][r:P:QUADRANT, :].bitcast(I32),
                in_=wh_scale_rows[r].bitcast(I32),
            )

        for n in range(GATES):
            if n != GATE_O:
                nc.sync.dma_start(out=bias_rows[0:1, n, :], in_=bx_in[n].unsqueeze(0))
                nc.sync.dma_start(out=bias_rows[1:2, n, :], in_=bh_in[n].unsqueeze(0))
                load_wh_scale(n, 0)
                load_wx(n, 0, BIG_CHUNK)
                load_wh_scale(n, 1)
                load_wh_scale(n, 2)
                load_wx(n, BIG_CHUNK, BIG_CHUNK)
                load_wh_scale(n, 3)
                load_wh(n)
            else:
                nc.sync.dma_start(out=bias_rows[0:1, n, :], in_=bx_in[n].unsqueeze(0))
                nc.sync.dma_start(out=bias_rows[1:2, n, :], in_=bh_in[n].unsqueeze(0))
                for r in range(QUADRANT_ROWS - 1):
                    load_wh_scale(n, r)
                    load_wx(n, r * CHUNK, CHUNK)
                load_wh_scale(n, QUADRANT_ROWS - 1)
                load_wh(n)
                for first, count in LATE_PIECES:
                    load_wx(n, first, count)

        xh_pairs = xh[:].bitcast(F32)
        banks_done = 0
        for first in range(0, PASSES, CHUNK):
            count = min(CHUNK, PASSES - first)
            grouped = stage.tile([P, CHUNK, P, PACK], BF16, align_bytes=64)
            for lead in range(0, count, BANK_PASSES):
                here = min(BANK_PASSES, count - lead)
                flipped = plain.tile([P, BANK_PASSES, PAIRS, P], F32, tag="plain")
                for j in range(here):
                    start = (first + lead + j) * PASS_WORDS
                    for u in range(PAIRS):
                        nc.tensor.transpose(
                            flipped[:, j, u, :],
                            xh_pairs[:, start + u : start + PASS_WORDS : PAIRS],
                            identity[:],
                        )
                copy_out = nc.vector.tensor_copy if banks_done % 2 == 0 else nc.scalar.copy
                copy_out(
                    out=grouped[:, lead : lead + here, :, :].bitcast(F32),
                    in_=flipped[:, 0:here, :, :].rearrange("p j u b -> p j b u"),
                )
                banks_done += 1
            nc.vector.quantize_mx(
                out=xh_codes[:, first : first + count, :]
                .rearrange("p g b -> p (g b)")
                .bitcast(FP8X4),
                scales=xh_planes[:, first : first + count, :].rearrange("p g b -> p (g b)"),
                in_=grouped[:, 0:count, :, :].rearrange("p g b t -> p (g b t)"),
            )

        gate = []
        for n in range(GATES):
            spread = plain.tile([P, DOUT], F32, tag="plain")
            nc.tensor.matmul(
                out=spread[:], lhsT=ones[:], rhs=bias_rows[:, n, :], start=True, stop=True
            )
            bias = keep.tile([P, DOUT], F32, name="bias_%d" % n)
            nc.scalar.copy(out=bias[:], in_=spread[:])

            def mx_pass(out, g, cols, start, stop):
                if g == H_PASS:
                    w_plane = wh_plane[n][:, cols]
                else:
                    w_plane = wx_planes[QUADRANT_ROWS * n : P, g, cols]
                nc.tensor.matmul_mx(
                    out=out,
                    lhsT=xh_codes[:, g, :].bitcast(FP8X4),
                    lhsT_scale=xh_planes[:, g, :],
                    rhs=w_words[n][:, g, cols].bitcast(FP8X4),
                    rhs_scale=w_plane,
                    start=start,
                    stop=stop,
                )

            z_sum = sums.tile([P, DOUT], F32, name="z_sum_%d" % n, tag="bank_%d" % n)
            if n == GATE_O:
                group = list(range(LATE_FIRST)) + [H_PASS]
            else:
                group = list(range(PASSES))
            for g in group:
                mx_pass(z_sum[:], g, slice(0, DOUT), g == group[0], g == group[-1])
            z = keep.tile([P, DOUT], F32, name="z_%d" % n)
            nc.vector.tensor_add(out=z[:], in0=z_sum[:], in1=bias[:])
            value = keep.tile([P, DOUT], F32, name="gate_%d" % n)
            if n != GATE_O:
                nc.scalar.activation(out=value[:], in_=z[:], func=GATE_FUNC[n])
            gate.append(value)

            if n == GATE_F:
                kept = keep.tile([P, DOUT], F32)
                nc.vector.tensor_mul(out=kept[:], in0=gate[GATE_F][:], in1=c_sb[:])
            if n == GATE_G:
                fresh = keep.tile([P, DOUT], F32)
                nc.vector.tensor_mul(out=fresh[:], in0=gate[GATE_I][:], in1=gate[GATE_G][:])
                c_new = keep.tile([P, DOUT], F32)
                nc.vector.tensor_add(out=c_new[:], in0=kept[:], in1=fresh[:])
                tanh_c = keep.tile([P, DOUT], F32)
                nc.scalar.activation(out=tanh_c[:], in_=c_new[:], func=ACT.Tanh)
                nc.sync.dma_start(out=out_1, in_=c_new[:])
            if n == GATE_O:
                halves = [slice(j * HALF, (j + 1) * HALF) for j in range(DOUT // HALF)]
                late = [
                    sums.tile([P, HALF], F32, name="late_%d" % j, tag="bank_%d" % j)
                    for j in range(len(halves))
                ]
                for g in range(LATE_FIRST, X_PASSES):
                    for j, cols in enumerate(halves):
                        mx_pass(late[j][:], g, cols, g == LATE_FIRST, g == X_PASSES - 1)
                z_whole = keep.tile([P, DOUT], F32)
                h_new = keep.tile([P, DOUT], F32)
                for j, cols in enumerate(halves):
                    nc.vector.tensor_add(out=z_whole[:, cols], in0=late[j][:], in1=z[:, cols])
                    nc.scalar.activation(
                        out=value[:, cols], in_=z_whole[:, cols], func=GATE_FUNC[n]
                    )
                for cols in halves:
                    nc.vector.tensor_mul(
                        out=h_new[:, cols], in0=value[:, cols], in1=tanh_c[:, cols]
                    )
                    nc.sync.dma_start(out=out_0[:, cols], in_=h_new[:, cols])
